import numpy as np
import ml_dtypes


def mxq(x, axis, fmt="e4m3"):
    dtype, down = {"e4m3": (ml_dtypes.float8_e4m3fn, 7), "e5m2": (ml_dtypes.float8_e5m2, 14)}[fmt]
    v = np.moveaxis(np.asarray(x, np.float32).astype(ml_dtypes.bfloat16).astype(np.float64), axis, -1)
    blocks = v.reshape(v.shape[:-1] + (-1, 32))
    amax = np.abs(blocks).max(-1, keepdims=True)
    byte = np.maximum(np.where(amax > 0, np.frexp(amax)[1] - 1 + 127, 0) - down, 1)
    scale = np.exp2(byte - 127.0)
    codes = (blocks / scale).astype(np.float32).astype(dtype).astype(np.float64)
    return np.moveaxis((codes * scale).reshape(v.shape), -1, axis)


WIDE = False


def mx_kscale(k):
    if not WIDE:
        return np.ones(k)
    levels = np.array([10, -10, 5, -5, 0])
    a = np.random.permutation(np.resize(levels, k // 512 * 4)).reshape(k // 512, 4)
    idx = np.arange(k)
    return np.exp2(a[idx // 512, idx % 128 // 32])


BF16 = ml_dtypes.bfloat16


def bf(x):
    return np.asarray(x, np.float32).astype(BF16)


def f64(x):
    return np.asarray(x).astype(np.float64)


B, T, H, KV, D = 4, 1024, 2, 1, 256
G = H // KV
NEG = -1e9


def setup_inputs():
    s = mx_kscale(T)
    keep = np.random.random((1, 1, T, T)) < 0.5
    mask_w = np.where(keep, 1.0 + 0.3 * np.random.standard_normal((1, 1, T, T)), 0.0)
    mask_b = np.where(keep, 0.5 * np.random.standard_normal((1, 1, T, T)) + np.log(s)[None, None, None, :], NEG)
    return {"q_rot": bf(np.random.standard_normal((B, T, H, D))),
            "k_rot": bf(np.random.standard_normal((B, T, KV, D))),
            "v": bf(np.random.standard_normal((B, T, KV, D)) * 2.0 * (s.max() / s)[None, :, None, None]),
            "mask_w": bf(mask_w), "mask_b": bf(mask_b)}


def reference(q_rot, k_rot, v, mask_w, mask_b):
    qg = f64(q_rot).transpose(0, 2, 1, 3).reshape(B, KV, G * T, D)
    kt = f64(k_rot).transpose(0, 2, 3, 1)
    s = (qg @ kt).reshape(B, H, T, T) * (1.0 / np.sqrt(D))
    s = s * f64(mask_w) + f64(mask_b)
    e = np.exp(s - s.max(-1, keepdims=True))
    eq = mxq(e.reshape(B, KV, G * T, T), 3, "e4m3")
    vq = mxq(f64(v).transpose(0, 2, 1, 3), 2, "e4m3")
    o = (eq @ vq).reshape(B, H, T, D) / e.sum(-1, keepdims=True)
    return o.transpose(0, 2, 1, 3)

@@ -1,0 +1,276 @@
+from contextlib import ExitStack
+
+import concourse.masks as masks
+import concourse.mybir as mybir
+
+F32 = mybir.dt.float32
+BF16 = mybir.dt.bfloat16
+U32 = mybir.dt.uint32
+U8 = mybir.dt.uint8
+FP8X4 = mybir.dt.float8_e4m3fn_x4
+ALU = mybir.AluOpType
+ACT = mybir.ActivationFunctionType
+AXIS = mybir.AxisListType
+
+B, T, H, D = 4, 1024, 2, 256
+P = 128
+BANK = 512
+PACK = 4
+PASSES = T // (P * PACK)
+QT = T // P
+DC = D // P
+HALVES = T // BANK
+PAIRS = B * QT
+SCORE_SCALE = 1.0 / 16.0
+KEY_QUARTERS = 4
+QUERY_LEAD = 4
+
+FLOPS = 2 * 2 * B * H * T * T * D
+
+
+def tile_mistralselfattention_pb_t_kernel(tc, q_rot, k_rot, v, mask_w, mask_b, out):
+    nc = tc.nc
+    with ExitStack() as ctx:
+        ctx.enter_context(tc.manual_schedule())
+        const = ctx.enter_context(tc.tile_pool(name="const", bufs=1))
+        mask_pool = ctx.enter_context(tc.tile_pool(name="masks", bufs=1))
+        raw = ctx.enter_context(tc.tile_pool(name="raw", bufs=B))
+        flipped_pool = ctx.enter_context(tc.tile_pool(name="flipped", bufs=2))
+        value_pool = ctx.enter_context(tc.tile_pool(name="values", bufs=2))
+        masked_pool = ctx.enter_context(tc.tile_pool(name="masked", bufs=3))
+        work = ctx.enter_context(tc.tile_pool(name="work", bufs=2))
+        small = ctx.enter_context(tc.tile_pool(name="small", bufs=4))
+        result_pool = ctx.enter_context(tc.tile_pool(name="result", bufs=3))
+        score_banks = ctx.enter_context(tc.psum_pool(name="score_banks", bufs=H * HALVES))
+        prob_banks = ctx.enter_context(tc.psum_pool(name="prob_banks", bufs=H))
+        out_banks = ctx.enter_context(tc.psum_pool(name="out_banks", bufs=1))
+        operand_banks = ctx.enter_context(tc.psum_pool(name="operand_banks", bufs=1))
+
+        ident_bf16 = const.tile([P, P], BF16)
+        masks.make_identity(nc, ident_bf16[:])
+        ident_f32 = const.tile([P, P], F32)
+        masks.make_identity(nc, ident_f32[:])
+
+        zero = const.tile([P, 1], F32)
+        nc.vector.memset(zero[:], 0.0)
+        one = const.tile([P, 1], F32)
+        nc.scalar.activation(out=one[:], in_=zero[:], func=ACT.Exp)
+
+        q_raw, k_raw, v_raw, weight_rows, bias_rows = {}, {}, {}, {}, {}
+
+        def load_keys(b):
+            k_raw[b] = raw.tile([P, QT, D], BF16, name="k_raw")
+            nc.sync.dma_start(out=k_raw[b][:], in_=k_rot[b].rearrange("(t p) o d -> p t (o d)", p=P))
+
+        def load_queries(b):
+            q_raw[b] = raw.tile([P, QT, H * D], BF16, name="q_raw")
+            nc.sync.dma_start(out=q_raw[b][:], in_=q_rot[b].rearrange("(t p) h d -> p t (h d)", p=P))
+
+        def load_values(b):
+            v_raw[b] = raw.tile([P, PASSES, PACK, D], BF16, name="v_raw")
+            nc.sync.dma_start(
+                out=v_raw[b][:].rearrange("p g (u e) d -> p (g u) (e d)", u=2),
+                in_=v[b].rearrange("(c p e) o d -> p c (e o d)", p=P, e=2),
+            )
+
+        def load_masks(qt):
+            rows = slice(qt * P, (qt + 1) * P)
+            weight_rows[qt] = mask_pool.tile([P, T], BF16, name="weight_rows%d" % qt)
+            nc.sync.dma_start(out=weight_rows[qt][:], in_=mask_w[0, 0, rows, :])
+            bias_rows[qt] = mask_pool.tile([P, T], BF16, name="bias_rows%d" % qt)
+            nc.sync.dma_start(out=bias_rows[qt][:], in_=mask_b[0, 0, rows, :])
+
+        load_keys(0)
+        load_queries(0)
+        load_masks(0)
+        load_values(0)
+        load_keys(1)
+        for qt in range(1, QT):
+            load_masks(qt)
+        load_queries(1)
+        load_values(1)
+        for b in range(2, B):
+            load_keys(b)
+            load_queries(b)
+            load_values(b)
+
+        q_flipped, k_flipped, v_grouped, v_codes, v_scales = {}, {}, {}, {}, {}
+        scores, masked, neg_max, row_sum, inv_sum = {}, {}, {}, {}, {}
+        probs, probs_flipped, probs_grouped, prob_codes, prob_scales, products = {}, {}, {}, {}, {}, {}
+
+        def live(pair):
+            return 0 <= pair < PAIRS
+
+        def flip_operands(step):
+            pair = step + QUERY_LEAD
+            next_b, quarter = step // QT + 1, step % QT
+            with_keys = quarter < KEY_QUARTERS and 0 <= next_b < B
+            if not (live(pair) or with_keys):
+                return
+            bank = operand_banks.tile([P, 2, DC, 2, P], BF16, name="operand_bank")
+            if live(pair):
+                b, qt = divmod(pair, QT)
+                if qt == 0:
+                    q_flipped[b] = flipped_pool.tile([P, DC, H, T], BF16, name="q_flipped")
+                for c in range(DC):
+                    for h in range(H):
+                        first = h * D + c * P
+                        nc.tensor.transpose(bank[:, 0, c, h, :], q_raw[b][:, qt, first : first + P], ident_bf16[:])
+                nc.scalar.copy(out=q_flipped[b][:, :, :, qt * P : (qt + 1) * P], in_=bank[:, 0])
+            if with_keys:
+                if quarter == 0:
+                    k_flipped[next_b] = flipped_pool.tile([P, DC, T], BF16, name="k_flipped")
+                for c in range(DC):
+                    for j in range(2):
+                        nc.tensor.transpose(
+                            bank[:, 1, c, j, :], k_raw[next_b][:, 2 * quarter + j, c * P : (c + 1) * P], ident_bf16[:]
+                        )
+                nc.scalar.copy(
+                    out=k_flipped[next_b][:, :, 2 * quarter * P : 2 * (quarter + 1) * P],
+                    in_=bank[:, 1].rearrange("p c j k -> p c (j k)"),
+                )
+
+        def group_values(b):
+            v_grouped[b] = value_pool.tile([P, PASSES, D, PACK], BF16, name="v_grouped", align_bytes=64)
+            nc.scalar.copy(out=v_grouped[b][:], in_=v_raw[b][:].rearrange("p g t d -> p g d t"))
+
+        def quantise_values(b):
+            v_codes[b] = value_pool.tile([P, PASSES, D], U32, name="v_codes", align_bytes=64)
+            v_scales[b] = value_pool.tile([P, PASSES, D], U8, name="v_scales", align_bytes=64)
+            nc.vector.quantize_mx(
+                out=v_codes[b][:].rearrange("p g d -> p (g d)").bitcast(FP8X4),
+                scales=v_scales[b][:].rearrange("p g d -> p (g d)"),
+                in_=v_grouped[b][:].rearrange("p g d t -> p (g d t)"),
+            )
+
+        def score_matmuls(pair):
+            b, qt = divmod(pair, QT)
+            for h in range(H):
+                for half in range(HALVES):
+                    bank = score_banks.tile([P, BANK], F32, name="score_bank")
+                    scores[(pair, h, half)] = bank
+                    for c in range(DC):
+                        nc.tensor.matmul(
+                            out=bank[:],
+                            lhsT=q_flipped[b][:, c, h, qt * P : (qt + 1) * P],
+                            rhs=k_flipped[b][:, c, half * BANK : (half + 1) * BANK],
+                            start=(c == 0),
+                            stop=(c == DC - 1),
+                        )
+
+        def weigh(pair):
+            qt = pair % QT
+            masked[pair] = masked_pool.tile([P, H, T], F32, name="masked")
+            for h in range(H):
+                for half in range(HALVES):
+                    keys = slice(half * BANK, (half + 1) * BANK)
+                    nc.vector.scalar_tensor_tensor(
+                        out=masked[pair][:, h, keys],
+                        in0=scores[(pair, h, half)][:],
+                        scalar=SCORE_SCALE,
+                        in1=weight_rows[qt][:, keys],
+                        op0=ALU.mult,
+                        op1=ALU.mult,
+                    )
+
+        def add_bias(pair):
+            qt = pair % QT
+            nc.gpsimd.tensor_tensor(
+                out=masked[pair][:],
+                in0=masked[pair][:],
+                in1=bias_rows[qt][:].unsqueeze(1).to_broadcast([P, H, T]),
+                op=ALU.add,
+            )
+
+        def row_maxima(pair):
+            neg_max[pair] = small.tile([P, H], F32, name="neg_max")
+            nc.vector.tensor_reduce(out=neg_max[pair][:], in_=masked[pair][:], axis=AXIS.X, op=ALU.max, negate=True)
+
+        def exponentials(pair):
+            probs[pair] = work.tile([P, H, T], BF16, name="probs")
+            row_sum[pair] = small.tile([P, H], F32, name="row_sum")
+            for h in range(H):
+                nc.scalar.activation(
+                    out=probs[pair][:, h, :],
+                    in_=masked[pair][:, h, :],
+                    func=ACT.Exp,
+                    bias=neg_max[pair][:, h : h + 1],
+                    scale=1.0,
+                    accum_out=row_sum[pair][:, h : h + 1],
+                )
+
+        def flip_probs(pair):
+            for h in range(H):
+                bank = prob_banks.tile([P, PASSES * 2, P], F32, name="prob_bank")
+                probs_flipped[(pair, h)] = bank
+                words = probs[pair][:, h, :].bitcast(F32)
+                for c in range(PASSES * 2):
+                    nc.tensor.transpose(bank[:, c, :], words[:, c * P : (c + 1) * P], ident_f32[:])
+
+        def group_probs(pair):
+            probs_grouped[pair] = work.tile([P, H, PASSES, P, PACK], BF16, name="probs_grouped", align_bytes=64)
+            for h in range(H):
+                nc.scalar.copy(
+                    out=probs_grouped[pair][:, h].bitcast(F32),
+                    in_=probs_flipped[(pair, h)][:].rearrange("p (g u) q -> p g q u", u=2),
+                )
+
+        def quantise_probs(pair):
+            prob_codes[pair] = work.tile([P, H, PASSES, P], U32, name="prob_codes", align_bytes=64)
+            prob_scales[pair] = work.tile([P, H, PASSES, P], U8, name="prob_scales", align_bytes=64)
+            nc.vector.quantize_mx(
+                out=prob_codes[pair][:].rearrange("p h g q -> p (h g q)").bitcast(FP8X4),
+                scales=prob_scales[pair][:].rearrange("p h g q -> p (h g q)"),
+                in_=probs_grouped[pair][:].rearrange("p h g q t -> p (h g q t)"),
+            )
+            inv_sum[pair] = small.tile([P, H], F32, name="inv_sum")
+            nc.vector.reciprocal(out=inv_sum[pair][:], in_=row_sum[pair][:])
+
+        def weighted_values(pair):
+            b = pair // QT
+            products[pair] = out_banks.tile([P, H, D], F32, name="out_bank")
+            for h in range(H):
+                for g in range(PASSES):
+                    nc.tensor.matmul_mx(
+                        out=products[pair][:, h, :],
+                        lhsT=prob_codes[pair][:, h, g, :].bitcast(FP8X4),
+                        lhsT_scale=prob_scales[pair][:, h, g, :],
+                        rhs=v_codes[b][:, g, :].bitcast(FP8X4),
+                        rhs_scale=v_scales[b][:, g, :],
+                        start=(g == 0),
+                        stop=(g == PASSES - 1),
+                    )
+
+        def normalise_and_store(pair):
+            b, qt = divmod(pair, QT)
+            result = result_pool.tile([P, H, D], F32, name="result")
+            for h in range(H):
+                nc.scalar.activation(
+                    out=result[:, h, :], in_=products[pair][:, h, :], func=ACT.Copy, scale=inv_sum[pair][:, h : h + 1]
+                )
+            nc.sync.dma_start(out=out[b, qt * P : (qt + 1) * P, :, :], in_=result[:])
+
+        for step in range(-QT, PAIRS + 2):
+            if live(step):
+                row_maxima(step)
+                exponentials(step)
+            if live(step - 2):
+                normalise_and_store(step - 2)
+            flip_operands(step)
+            if (step + 1) % QT == 0 and live(step + 1):
+                group_values((step + 1) // QT)
+            if live(step + 2):
+                weigh(step + 2)
+            if live(step + 3):
+                score_matmuls(step + 3)
+            if live(step + 1):
+                add_bias(step + 1)
+            if live(step - 1):
+                quantise_probs(step - 1)
+            if step % QT == 0 and live(step):
+                quantise_values(step // QT)
+            if live(step):
+                flip_probs(step)
+                group_probs(step)
+            if live(step - 1):
+                weighted_values(step - 1)

@@ -24,6 +24,8 @@ PAIRS = B * QT
 SCORE_SCALE = 1.0 / 16.0
 KEY_QUARTERS = 4
 QUERY_LEAD = 4
+SCORE_LEAD = 3
+FIRST_SCORE_STEP = -SCORE_LEAD
 
 FLOPS = 2 * 2 * B * H * T * T * D
 
@@ -107,7 +109,10 @@ def tile_mistralselfattention_pb_t_kernel(tc, q_rot, k_rot, v, mask_w, mask_b, o
             with_keys = quarter < KEY_QUARTERS and 0 <= next_b < B
             if not (live(pair) or with_keys):
                 return
-            bank = operand_banks.tile([P, 2, DC, 2, P], BF16, name="operand_bank")
+            if step < FIRST_SCORE_STEP:
+                bank = score_banks.tile([P, 2, DC, 2, P], BF16, name="early_operand_bank", tag="score_bank")
+            else:
+                bank = operand_banks.tile([P, 2, DC, 2, P], BF16, name="operand_bank")
             if live(pair):
                 b, qt = divmod(pair, QT)
                 if qt == 0:
@@ -250,27 +255,28 @@ def tile_mistralselfattention_pb_t_kernel(tc, q_rot, k_rot, v, mask_w, mask_b, o
                 )
             nc.sync.dma_start(out=out[b, qt * P : (qt + 1) * P, :, :], in_=result[:])
 
-        for step in range(-QT, PAIRS + 2):
+        for step in range(-QT, PAIRS + 3):
             if live(step):
                 row_maxima(step)
                 exponentials(step)
-            if live(step - 2):
-                normalise_and_store(step - 2)
+            if live(step - 1):
+                group_probs(step - 1)
+            if live(step - 3):
+                normalise_and_store(step - 3)
             flip_operands(step)
             if (step + 1) % QT == 0 and live(step + 1):
                 group_values((step + 1) // QT)
             if live(step + 2):
                 weigh(step + 2)
-            if live(step + 3):
-                score_matmuls(step + 3)
+            if live(step + SCORE_LEAD):
+                score_matmuls(step + SCORE_LEAD)
             if live(step + 1):
                 add_bias(step + 1)
-            if live(step - 1):
-                quantise_probs(step - 1)
+            if live(step - 2):
+                quantise_probs(step - 2)
             if step % QT == 0 and live(step):
                 quantise_values(step // QT)
             if live(step):
                 flip_probs(step)
-                group_probs(step)
-            if live(step - 1):
-                weighted_values(step - 1)
+            if live(step - 2):
+                weighted_values(step - 2)

@@ -23,8 +23,9 @@ HALVES = T // BANK
 PAIRS = B * QT
 SCORE_SCALE = 1.0 / 16.0
 KEY_QUARTERS = 4
-QUERY_LEAD = 4
-SCORE_LEAD = 3
+QUERY_LEAD = 5
+SCORE_LEAD = 4
+WEIGH_LEAD = 3
 FIRST_SCORE_STEP = -SCORE_LEAD
 
 FLOPS = 2 * 2 * B * H * T * T * D
@@ -33,13 +34,12 @@ FLOPS = 2 * 2 * B * H * T * T * D
 def tile_mistralselfattention_pb_t_kernel(tc, q_rot, k_rot, v, mask_w, mask_b, out):
     nc = tc.nc
     with ExitStack() as ctx:
-        ctx.enter_context(tc.manual_schedule())
         const = ctx.enter_context(tc.tile_pool(name="const", bufs=1))
         mask_pool = ctx.enter_context(tc.tile_pool(name="masks", bufs=1))
         raw = ctx.enter_context(tc.tile_pool(name="raw", bufs=B))
         flipped_pool = ctx.enter_context(tc.tile_pool(name="flipped", bufs=2))
         value_pool = ctx.enter_context(tc.tile_pool(name="values", bufs=2))
-        masked_pool = ctx.enter_context(tc.tile_pool(name="masked", bufs=3))
+        masked_pool = ctx.enter_context(tc.tile_pool(name="masked", bufs=WEIGH_LEAD + 1))
         work = ctx.enter_context(tc.tile_pool(name="work", bufs=2))
         small = ctx.enter_context(tc.tile_pool(name="small", bufs=4))
         result_pool = ctx.enter_context(tc.tile_pool(name="result", bufs=3))
@@ -84,10 +84,11 @@ def tile_mistralselfattention_pb_t_kernel(tc, q_rot, k_rot, v, mask_w, mask_b, o
 
         load_keys(0)
         load_queries(0)
-        load_masks(0)
+        for qt in range(WEIGH_LEAD):
+            load_masks(qt)
         load_values(0)
         load_keys(1)
-        for qt in range(1, QT):
+        for qt in range(WEIGH_LEAD, QT):
             load_masks(qt)
         load_queries(1)
         load_values(1)
@@ -266,8 +267,8 @@ def tile_mistralselfattention_pb_t_kernel(tc, q_rot, k_rot, v, mask_w, mask_b, o
             flip_operands(step)
             if (step + 1) % QT == 0 and live(step + 1):
                 group_values((step + 1) // QT)
-            if live(step + 2):
-                weigh(step + 2)
+            if live(step + WEIGH_LEAD):
+                weigh(step + WEIGH_LEAD)
             if live(step + SCORE_LEAD):
                 score_matmuls(step + SCORE_LEAD)
             if live(step + 1):

@@ -21,11 +21,11 @@ QT = T // P
 DC = D // P
 HALVES = T // BANK
 PAIRS = B * QT
+DUO = 2
 SCORE_SCALE = 1.0 / 16.0
 KEY_QUARTERS = 4
-QUERY_LEAD = 5
-SCORE_LEAD = 4
-WEIGH_LEAD = 3
+QUERY_LEAD = 4
+SCORE_LEAD = 3
 FIRST_SCORE_STEP = -SCORE_LEAD
 
 FLOPS = 2 * 2 * B * H * T * T * D
@@ -34,12 +34,13 @@ FLOPS = 2 * 2 * B * H * T * T * D
 def tile_mistralselfattention_pb_t_kernel(tc, q_rot, k_rot, v, mask_w, mask_b, out):
     nc = tc.nc
     with ExitStack() as ctx:
+        ctx.enter_context(tc.manual_schedule())
         const = ctx.enter_context(tc.tile_pool(name="const", bufs=1))
         mask_pool = ctx.enter_context(tc.tile_pool(name="masks", bufs=1))
         raw = ctx.enter_context(tc.tile_pool(name="raw", bufs=B))
         flipped_pool = ctx.enter_context(tc.tile_pool(name="flipped", bufs=2))
         value_pool = ctx.enter_context(tc.tile_pool(name="values", bufs=2))
-        masked_pool = ctx.enter_context(tc.tile_pool(name="masked", bufs=WEIGH_LEAD + 1))
+        masked_pool = ctx.enter_context(tc.tile_pool(name="masked", bufs=3))
         work = ctx.enter_context(tc.tile_pool(name="work", bufs=2))
         small = ctx.enter_context(tc.tile_pool(name="small", bufs=4))
         result_pool = ctx.enter_context(tc.tile_pool(name="result", bufs=3))
@@ -84,11 +85,10 @@ def tile_mistralselfattention_pb_t_kernel(tc, q_rot, k_rot, v, mask_w, mask_b, o
 
         load_keys(0)
         load_queries(0)
-        for qt in range(WEIGH_LEAD):
-            load_masks(qt)
+        load_masks(0)
         load_values(0)
         load_keys(1)
-        for qt in range(WEIGH_LEAD, QT):
+        for qt in range(1, QT):
             load_masks(qt)
         load_queries(1)
         load_values(1)
@@ -181,7 +181,8 @@ def tile_mistralselfattention_pb_t_kernel(tc, q_rot, k_rot, v, mask_w, mask_b, o
 
         def add_bias(pair):
             qt = pair % QT
-            nc.gpsimd.tensor_tensor(
+            engine = nc.vector if pair in (0, PAIRS - 1) else nc.gpsimd
+            engine.tensor_tensor(
                 out=masked[pair][:],
                 in0=masked[pair][:],
                 in1=bias_rows[qt][:].unsqueeze(1).to_broadcast([P, H, T]),
@@ -193,8 +194,10 @@ def tile_mistralselfattention_pb_t_kernel(tc, q_rot, k_rot, v, mask_w, mask_b, o
             nc.vector.tensor_reduce(out=neg_max[pair][:], in_=masked[pair][:], axis=AXIS.X, op=ALU.max, negate=True)
 
         def exponentials(pair):
+            duo, member = divmod(pair, DUO)
             probs[pair] = work.tile([P, H, T], BF16, name="probs")
-            row_sum[pair] = small.tile([P, H], F32, name="row_sum")
+            if member == 0:
+                row_sum[duo] = small.tile([P, DUO, H], F32, name="row_sum")
             for h in range(H):
                 nc.scalar.activation(
                     out=probs[pair][:, h, :],
@@ -202,7 +205,7 @@ def tile_mistralselfattention_pb_t_kernel(tc, q_rot, k_rot, v, mask_w, mask_b, o
                     func=ACT.Exp,
                     bias=neg_max[pair][:, h : h + 1],
                     scale=1.0,
-                    accum_out=row_sum[pair][:, h : h + 1],
+                    accum_out=row_sum[duo][:, member, h : h + 1],
                 )
 
         def flip_probs(pair):
@@ -214,33 +217,36 @@ def tile_mistralselfattention_pb_t_kernel(tc, q_rot, k_rot, v, mask_w, mask_b, o
                     nc.tensor.transpose(bank[:, c, :], words[:, c * P : (c + 1) * P], ident_f32[:])
 
         def group_probs(pair):
-            probs_grouped[pair] = work.tile([P, H, PASSES, P, PACK], BF16, name="probs_grouped", align_bytes=64)
+            duo, member = divmod(pair, DUO)
+            if member == 0:
+                probs_grouped[duo] = work.tile([P, DUO, H, PASSES, P, PACK], BF16, name="probs_grouped", align_bytes=64)
             for h in range(H):
                 nc.scalar.copy(
-                    out=probs_grouped[pair][:, h].bitcast(F32),
+                    out=probs_grouped[duo][:, member, h].bitcast(F32),
                     in_=probs_flipped[(pair, h)][:].rearrange("p (g u) q -> p g q u", u=2),
                 )
 
-        def quantise_probs(pair):
-            prob_codes[pair] = work.tile([P, H, PASSES, P], U32, name="prob_codes", align_bytes=64)
-            prob_scales[pair] = work.tile([P, H, PASSES, P], U8, name="prob_scales", align_bytes=64)
+        def quantise_probs(duo):
+            prob_codes[duo] = work.tile([P, DUO, H, PASSES, P], U32, name="prob_codes", align_bytes=64)
+            prob_scales[duo] = work.tile([P, DUO, H, PASSES, P], U8, name="prob_scales", align_bytes=64)
             nc.vector.quantize_mx(
-                out=prob_codes[pair][:].rearrange("p h g q -> p (h g q)").bitcast(FP8X4),
-                scales=prob_scales[pair][:].rearrange("p h g q -> p (h g q)"),
-                in_=probs_grouped[pair][:].rearrange("p h g q t -> p (h g q t)"),
+                out=prob_codes[duo][:].rearrange("p a h g q -> p (a h g q)").bitcast(FP8X4),
+                scales=prob_scales[duo][:].rearrange("p a h g q -> p (a h g q)"),
+                in_=probs_grouped[duo][:].rearrange("p a h g q t -> p (a h g q t)"),
             )
-            inv_sum[pair] = small.tile([P, H], F32, name="inv_sum")
-            nc.vector.reciprocal(out=inv_sum[pair][:], in_=row_sum[pair][:])
+            inv_sum[duo] = small.tile([P, DUO, H], F32, name="inv_sum")
+            nc.vector.reciprocal(out=inv_sum[duo][:], in_=row_sum[duo][:])
 
         def weighted_values(pair):
             b = pair // QT
+            duo, member = divmod(pair, DUO)
             products[pair] = out_banks.tile([P, H, D], F32, name="out_bank")
             for h in range(H):
                 for g in range(PASSES):
                     nc.tensor.matmul_mx(
                         out=products[pair][:, h, :],
-                        lhsT=prob_codes[pair][:, h, g, :].bitcast(FP8X4),
-                        lhsT_scale=prob_scales[pair][:, h, g, :],
+                        lhsT=prob_codes[duo][:, member, h, g, :].bitcast(FP8X4),
+                        lhsT_scale=prob_scales[duo][:, member, h, g, :],
                         rhs=v_codes[b][:, g, :].bitcast(FP8X4),
                         rhs_scale=v_scales[b][:, g, :],
                         start=(g == 0),
@@ -249,35 +255,39 @@ def tile_mistralselfattention_pb_t_kernel(tc, q_rot, k_rot, v, mask_w, mask_b, o
 
         def normalise_and_store(pair):
             b, qt = divmod(pair, QT)
+            duo, member = divmod(pair, DUO)
             result = result_pool.tile([P, H, D], F32, name="result")
             for h in range(H):
                 nc.scalar.activation(
-                    out=result[:, h, :], in_=products[pair][:, h, :], func=ACT.Copy, scale=inv_sum[pair][:, h : h + 1]
+                    out=result[:, h, :],
+                    in_=products[pair][:, h, :],
+                    func=ACT.Copy,
+                    scale=inv_sum[duo][:, member, h : h + 1],
                 )
             nc.sync.dma_start(out=out[b, qt * P : (qt + 1) * P, :, :], in_=result[:])
 
-        for step in range(-QT, PAIRS + 3):
+        for step in range(-QT, PAIRS + 4):
             if live(step):
                 row_maxima(step)
                 exponentials(step)
             if live(step - 1):
                 group_probs(step - 1)
-            if live(step - 3):
-                normalise_and_store(step - 3)
+            if live(step - 4):
+                normalise_and_store(step - 4)
             flip_operands(step)
             if (step + 1) % QT == 0 and live(step + 1):
                 group_values((step + 1) // QT)
-            if live(step + WEIGH_LEAD):
-                weigh(step + WEIGH_LEAD)
+            if live(step + 2):
+                weigh(step + 2)
             if live(step + SCORE_LEAD):
                 score_matmuls(step + SCORE_LEAD)
             if live(step + 1):
                 add_bias(step + 1)
-            if live(step - 2):
-                quantise_probs(step - 2)
+            if live(step - 2) and (step - 2) % DUO == DUO - 1:
+                quantise_probs((step - 2) // DUO)
             if step % QT == 0 and live(step):
                 quantise_values(step // QT)
             if live(step):
                 flip_probs(step)
-            if live(step - 2):
-                weighted_values(step - 2)
+            if live(step - 3):
+                weighted_values(step - 3)

from contextlib import ExitStack

import concourse.masks as masks
import concourse.mybir as mybir

F32 = mybir.dt.float32
BF16 = mybir.dt.bfloat16
U32 = mybir.dt.uint32
U8 = mybir.dt.uint8
FP8X4 = mybir.dt.float8_e4m3fn_x4
ALU = mybir.AluOpType
ACT = mybir.ActivationFunctionType
AXIS = mybir.AxisListType

B, T, H, D = 4, 1024, 2, 256
P = 128
BANK = 512
PACK = 4
PASSES = T // (P * PACK)
QT = T // P
DC = D // P
HALVES = T // BANK
PAIRS = B * QT
DUO = 2
SCORE_SCALE = 1.0 / 16.0
KEY_QUARTERS = 4
QUERY_LEAD = 4
SCORE_LEAD = 3
FIRST_SCORE_STEP = -SCORE_LEAD

FLOPS = 2 * 2 * B * H * T * T * D


def tile_mistralselfattention_pb_t_kernel(tc, q_rot, k_rot, v, mask_w, mask_b, out):
    nc = tc.nc
    with ExitStack() as ctx:
        ctx.enter_context(tc.manual_schedule())
        const = ctx.enter_context(tc.tile_pool(name="const", bufs=1))
        mask_pool = ctx.enter_context(tc.tile_pool(name="masks", bufs=1))
        raw = ctx.enter_context(tc.tile_pool(name="raw", bufs=B))
        flipped_pool = ctx.enter_context(tc.tile_pool(name="flipped", bufs=2))
        value_pool = ctx.enter_context(tc.tile_pool(name="values", bufs=2))
        masked_pool = ctx.enter_context(tc.tile_pool(name="masked", bufs=3))
        work = ctx.enter_context(tc.tile_pool(name="work", bufs=2))
        small = ctx.enter_context(tc.tile_pool(name="small", bufs=4))
        result_pool = ctx.enter_context(tc.tile_pool(name="result", bufs=3))
        score_banks = ctx.enter_context(tc.psum_pool(name="score_banks", bufs=H * HALVES))
        prob_banks = ctx.enter_context(tc.psum_pool(name="prob_banks", bufs=H))
        out_banks = ctx.enter_context(tc.psum_pool(name="out_banks", bufs=1))
        operand_banks = ctx.enter_context(tc.psum_pool(name="operand_banks", bufs=1))

        ident_bf16 = const.tile([P, P], BF16)
        masks.make_identity(nc, ident_bf16[:])
        ident_f32 = const.tile([P, P], F32)
        masks.make_identity(nc, ident_f32[:])

        zero = const.tile([P, 1], F32)
        nc.vector.memset(zero[:], 0.0)
        one = const.tile([P, 1], F32)
        nc.scalar.activation(out=one[:], in_=zero[:], func=ACT.Exp)

        q_raw, k_raw, v_raw, weight_rows, bias_rows = {}, {}, {}, {}, {}

        def load_keys(b):
            k_raw[b] = raw.tile([P, QT, D], BF16, name="k_raw")
            nc.sync.dma_start(out=k_raw[b][:], in_=k_rot[b].rearrange("(t p) o d -> p t (o d)", p=P))

        def load_queries(b):
            q_raw[b] = raw.tile([P, QT, H * D], BF16, name="q_raw")
            nc.sync.dma_start(out=q_raw[b][:], in_=q_rot[b].rearrange("(t p) h d -> p t (h d)", p=P))

        def load_values(b):
            v_raw[b] = raw.tile([P, PASSES, PACK, D], BF16, name="v_raw")
            nc.sync.dma_start(
                out=v_raw[b][:].rearrange("p g (u e) d -> p (g u) (e d)", u=2),
                in_=v[b].rearrange("(c p e) o d -> p c (e o d)", p=P, e=2),
            )

        def load_masks(qt):
            rows = slice(qt * P, (qt + 1) * P)
            weight_rows[qt] = mask_pool.tile([P, T], BF16, name="weight_rows%d" % qt)
            nc.sync.dma_start(out=weight_rows[qt][:], in_=mask_w[0, 0, rows, :])
            bias_rows[qt] = mask_pool.tile([P, T], BF16, name="bias_rows%d" % qt)
            nc.sync.dma_start(out=bias_rows[qt][:], in_=mask_b[0, 0, rows, :])

        load_keys(0)
        load_queries(0)
        load_masks(0)
        load_values(0)
        load_keys(1)
        for qt in range(1, QT):
            load_masks(qt)
        load_queries(1)
        load_values(1)
        for b in range(2, B):
            load_keys(b)
            load_queries(b)
            load_values(b)

        q_flipped, k_flipped, v_grouped, v_codes, v_scales = {}, {}, {}, {}, {}
        scores, masked, neg_max, row_sum, inv_sum = {}, {}, {}, {}, {}
        probs, probs_flipped, probs_grouped, prob_codes, prob_scales, products = {}, {}, {}, {}, {}, {}

        def live(pair):
            return 0 <= pair < PAIRS

        def flip_operands(step):
            pair = step + QUERY_LEAD
            next_b, quarter = step // QT + 1, step % QT
            with_keys = quarter < KEY_QUARTERS and 0 <= next_b < B
            if not (live(pair) or with_keys):
                return
            if step < FIRST_SCORE_STEP:
                bank = score_banks.tile([P, 2, DC, 2, P], BF16, name="early_operand_bank", tag="score_bank")
            else:
                bank = operand_banks.tile([P, 2, DC, 2, P], BF16, name="operand_bank")
            if live(pair):
                b, qt = divmod(pair, QT)
                if qt == 0:
                    q_flipped[b] = flipped_pool.tile([P, DC, H, T], BF16, name="q_flipped")
                for c in range(DC):
                    for h in range(H):
                        first = h * D + c * P
                        nc.tensor.transpose(bank[:, 0, c, h, :], q_raw[b][:, qt, first : first + P], ident_bf16[:])
                nc.scalar.copy(out=q_flipped[b][:, :, :, qt * P : (qt + 1) * P], in_=bank[:, 0])
            if with_keys:
                if quarter == 0:
                    k_flipped[next_b] = flipped_pool.tile([P, DC, T], BF16, name="k_flipped")
                for c in range(DC):
                    for j in range(2):
                        nc.tensor.transpose(
                            bank[:, 1, c, j, :], k_raw[next_b][:, 2 * quarter + j, c * P : (c + 1) * P], ident_bf16[:]
                        )
                nc.scalar.copy(
                    out=k_flipped[next_b][:, :, 2 * quarter * P : 2 * (quarter + 1) * P],
                    in_=bank[:, 1].rearrange("p c j k -> p c (j k)"),
                )

        def group_values(b):
            v_grouped[b] = value_pool.tile([P, PASSES, D, PACK], BF16, name="v_grouped", align_bytes=64)
            nc.scalar.copy(out=v_grouped[b][:], in_=v_raw[b][:].rearrange("p g t d -> p g d t"))

        def quantise_values(b):
            v_codes[b] = value_pool.tile([P, PASSES, D], U32, name="v_codes", align_bytes=64)
            v_scales[b] = value_pool.tile([P, PASSES, D], U8, name="v_scales", align_bytes=64)
            nc.vector.quantize_mx(
                out=v_codes[b][:].rearrange("p g d -> p (g d)").bitcast(FP8X4),
                scales=v_scales[b][:].rearrange("p g d -> p (g d)"),
                in_=v_grouped[b][:].rearrange("p g d t -> p (g d t)"),
            )

        def score_matmuls(pair):
            b, qt = divmod(pair, QT)
            for h in range(H):
                for half in range(HALVES):
                    bank = score_banks.tile([P, BANK], F32, name="score_bank")
                    scores[(pair, h, half)] = bank
                    for c in range(DC):
                        nc.tensor.matmul(
                            out=bank[:],
                            lhsT=q_flipped[b][:, c, h, qt * P : (qt + 1) * P],
                            rhs=k_flipped[b][:, c, half * BANK : (half + 1) * BANK],
                            start=(c == 0),
                            stop=(c == DC - 1),
                        )

        def weigh(pair):
            qt = pair % QT
            masked[pair] = masked_pool.tile([P, H, T], F32, name="masked")
            for h in range(H):
                for half in range(HALVES):
                    keys = slice(half * BANK, (half + 1) * BANK)
                    nc.vector.scalar_tensor_tensor(
                        out=masked[pair][:, h, keys],
                        in0=scores[(pair, h, half)][:],
                        scalar=SCORE_SCALE,
                        in1=weight_rows[qt][:, keys],
                        op0=ALU.mult,
                        op1=ALU.mult,
                    )

        def add_bias(pair):
            qt = pair % QT
            engine = nc.vector if pair in (0, PAIRS - 1) else nc.gpsimd
            engine.tensor_tensor(
                out=masked[pair][:],
                in0=masked[pair][:],
                in1=bias_rows[qt][:].unsqueeze(1).to_broadcast([P, H, T]),
                op=ALU.add,
            )

        def row_maxima(pair):
            neg_max[pair] = small.tile([P, H], F32, name="neg_max")
            nc.vector.tensor_reduce(out=neg_max[pair][:], in_=masked[pair][:], axis=AXIS.X, op=ALU.max, negate=True)

        def exponentials(pair):
            duo, member = divmod(pair, DUO)
            probs[pair] = work.tile([P, H, T], BF16, name="probs")
            if member == 0:
                row_sum[duo] = small.tile([P, DUO, H], F32, name="row_sum")
            for h in range(H):
                nc.scalar.activation(
                    out=probs[pair][:, h, :],
                    in_=masked[pair][:, h, :],
                    func=ACT.Exp,
                    bias=neg_max[pair][:, h : h + 1],
                    scale=1.0,
                    accum_out=row_sum[duo][:, member, h : h + 1],
                )

        def flip_probs(pair):
            for h in range(H):
                bank = prob_banks.tile([P, PASSES * 2, P], F32, name="prob_bank")
                probs_flipped[(pair, h)] = bank
                words = probs[pair][:, h, :].bitcast(F32)
                for c in range(PASSES * 2):
                    nc.tensor.transpose(bank[:, c, :], words[:, c * P : (c + 1) * P], ident_f32[:])

        def group_probs(pair):
            duo, member = divmod(pair, DUO)
            if member == 0:
                probs_grouped[duo] = work.tile([P, DUO, H, PASSES, P, PACK], BF16, name="probs_grouped", align_bytes=64)
            for h in range(H):
                nc.scalar.copy(
                    out=probs_grouped[duo][:, member, h].bitcast(F32),
                    in_=probs_flipped[(pair, h)][:].rearrange("p (g u) q -> p g q u", u=2),
                )

        def quantise_probs(duo):
            prob_codes[duo] = work.tile([P, DUO, H, PASSES, P], U32, name="prob_codes", align_bytes=64)
            prob_scales[duo] = work.tile([P, DUO, H, PASSES, P], U8, name="prob_scales", align_bytes=64)
            nc.vector.quantize_mx(
                out=prob_codes[duo][:].rearrange("p a h g q -> p (a h g q)").bitcast(FP8X4),
                scales=prob_scales[duo][:].rearrange("p a h g q -> p (a h g q)"),
                in_=probs_grouped[duo][:].rearrange("p a h g q t -> p (a h g q t)"),
            )
            inv_sum[duo] = small.tile([P, DUO, H], F32, name="inv_sum")
            nc.vector.reciprocal(out=inv_sum[duo][:], in_=row_sum[duo][:])

        def weighted_values(pair):
            b = pair // QT
            duo, member = divmod(pair, DUO)
            products[pair] = out_banks.tile([P, H, D], F32, name="out_bank")
            for h in range(H):
                for g in range(PASSES):
                    nc.tensor.matmul_mx(
                        out=products[pair][:, h, :],
                        lhsT=prob_codes[duo][:, member, h, g, :].bitcast(FP8X4),
                        lhsT_scale=prob_scales[duo][:, member, h, g, :],
                        rhs=v_codes[b][:, g, :].bitcast(FP8X4),
                        rhs_scale=v_scales[b][:, g, :],
                        start=(g == 0),
                        stop=(g == PASSES - 1),
                    )

        def normalise_and_store(pair):
            b, qt = divmod(pair, QT)
            duo, member = divmod(pair, DUO)
            result = result_pool.tile([P, H, D], F32, name="result")
            for h in range(H):
                nc.scalar.activation(
                    out=result[:, h, :],
                    in_=products[pair][:, h, :],
                    func=ACT.Copy,
                    scale=inv_sum[duo][:, member, h : h + 1],
                )
            nc.sync.dma_start(out=out[b, qt * P : (qt + 1) * P, :, :], in_=result[:])

        for step in range(-QT, PAIRS + 4):
            if live(step):
                row_maxima(step)
                exponentials(step)
            if live(step - 1):
                group_probs(step - 1)
            if live(step - 4):
                normalise_and_store(step - 4)
            flip_operands(step)
            if (step + 1) % QT == 0 and live(step + 1):
                group_values((step + 1) // QT)
            if live(step + 2):
                weigh(step + 2)
            if live(step + SCORE_LEAD):
                score_matmuls(step + SCORE_LEAD)
            if live(step + 1):
                add_bias(step + 1)
            if live(step - 2) and (step - 2) % DUO == DUO - 1:
                quantise_probs((step - 2) // DUO)
            if step % QT == 0 and live(step):
                quantise_values(step // QT)
            if live(step):
                flip_probs(step)
            if live(step - 3):
                weighted_values(step - 3)
